import numpy as np
import ml_dtypes

BF16 = ml_dtypes.bfloat16


def bf(x):
    return np.asarray(x, np.float32).astype(BF16)


def f32(x):
    return np.asarray(x, np.float32)


def f64(x):
    return np.asarray(x).astype(np.float64)


def striped(idx):
    return np.tile(idx.reshape(-1, 16).T, (8, 1))


D, S, N, K = 256, 4096, 2048, 2
EMA = 0.99
ZSCALE = 8.0


def setup_inputs():
    return {"base": f32(np.random.standard_normal((D, S))), "old": f32(np.random.standard_normal((D, N))), "za": f32(ZSCALE * np.random.standard_normal((D, N))), "zb": f32(ZSCALE * np.random.standard_normal((D, N))), "offs": striped(np.random.permutation(S)[:N])}


def reference(base, old, za, zb, offs):
    idx = offs[:16].T.reshape(-1)
    mean = (f64(za) + f64(zb)) * (1.0 / K)
    out = f64(base).copy()
    out[:, idx] = EMA * f64(old) + (1.0 - EMA) * mean
    return out

@@ -1,0 +1,45 @@
+import concourse.mybir as mybir
+
+F32 = mybir.dt.float32
+U16 = mybir.dt.uint16
+ADD = mybir.AluOpType.add
+
+P = 128
+D, S, N, K = 256, 4096, 2048, 2
+EMA = 0.99
+
+BYTES = 4 * D * (S - N) + 3 * 4 * D * N + 2 * P * (N // 16) + 4 * D * S
+
+
+def tile_httnbasehead_kernel(tc, base, old, za, zb, offs, out):
+    nc = tc.nc
+    n_blocks = D // P
+    with (
+        tc.tile_pool(name="held", bufs=1) as held,
+        tc.tile_pool(name="blocks", bufs=n_blocks) as blocks,
+    ):
+        offsets = held.tile([P, N // 16], U16, name="offsets")
+        nc.sync.dma_start(offsets[:], offs)
+
+        for b in range(n_blocks):
+            rows = slice(b * P, (b + 1) * P)
+
+            first = blocks.tile([P, N], F32, name="first")
+            second = blocks.tile([P, N], F32, name="second")
+            stale = blocks.tile([P, N], F32, name="stale")
+            window = blocks.tile([P, S], F32, name="window")
+            nc.sync.dma_start(first[:], za[rows, :])
+            nc.sync.dma_start(second[:], zb[rows, :])
+            nc.sync.dma_start(stale[:], old[rows, :])
+            nc.sync.dma_start(window[:], base[rows, :])
+
+            pair_sum = blocks.tile([P, N], F32, name="pair_sum")
+            mean_term = blocks.tile([P, N], F32, name="mean_term")
+            nc.vector.tensor_tensor(pair_sum[:], first[:], second[:], ADD)
+            nc.scalar.mul(mean_term[:], pair_sum[:], (1.0 - EMA) / K)
+
+            old_term = blocks.tile([P, N], F32, name="old_term")
+            nc.scalar.mul(old_term[:], stale[:], EMA)
+
+            nc.vector.tensor_tensor(window[:].indirect(offsets[:]), old_term[:], mean_term[:], ADD)
+            nc.sync.dma_start(out[rows, :], window[:])

@@ -3,6 +3,7 @@ import concourse.mybir as mybir
 F32 = mybir.dt.float32
 U16 = mybir.dt.uint16
 ADD = mybir.AluOpType.add
+MULT = mybir.AluOpType.mult
 
 P = 128
 D, S, N, K = 256, 4096, 2048, 2
@@ -14,6 +15,7 @@ BYTES = 4 * D * (S - N) + 3 * 4 * D * N + 2 * P * (N // 16) + 4 * D * S
 def tile_httnbasehead_kernel(tc, base, old, za, zb, offs, out):
     nc = tc.nc
     n_blocks = D // P
+    share = (1.0 - EMA) / K
     with (
         tc.tile_pool(name="held", bufs=1) as held,
         tc.tile_pool(name="blocks", bufs=n_blocks) as blocks,
@@ -21,25 +23,28 @@ def tile_httnbasehead_kernel(tc, base, old, za, zb, offs, out):
         offsets = held.tile([P, N // 16], U16, name="offsets")
         nc.sync.dma_start(offsets[:], offs)
 
+        first, second, stale, window = [], [], [], []
         for b in range(n_blocks):
             rows = slice(b * P, (b + 1) * P)
+            first.append(blocks.tile([P, N], F32, name="first"))
+            second.append(blocks.tile([P, N], F32, name="second"))
+            stale.append(blocks.tile([P, N], F32, name="stale"))
+            window.append(blocks.tile([P, S], F32, name="window"))
+            nc.sync.dma_start(first[b][:], za[rows, :])
+            nc.sync.dma_start(second[b][:], zb[rows, :])
+            nc.sync.dma_start(stale[b][:], old[rows, :])
+            nc.sync.dma_start(window[b][:], base[rows, :])
 
-            first = blocks.tile([P, N], F32, name="first")
-            second = blocks.tile([P, N], F32, name="second")
-            stale = blocks.tile([P, N], F32, name="stale")
-            window = blocks.tile([P, S], F32, name="window")
-            nc.sync.dma_start(first[:], za[rows, :])
-            nc.sync.dma_start(second[:], zb[rows, :])
-            nc.sync.dma_start(stale[:], old[rows, :])
-            nc.sync.dma_start(window[:], base[rows, :])
+        first_share, old_term = [], []
+        for b in range(n_blocks):
+            first_share.append(blocks.tile([P, N], F32, name="first_share"))
+            old_term.append(blocks.tile([P, N], F32, name="old_term"))
+            nc.scalar.mul(first_share[b][:], first[b][:], share)
+            nc.scalar.mul(old_term[b][:], stale[b][:], EMA)
 
-            pair_sum = blocks.tile([P, N], F32, name="pair_sum")
+        for b in range(n_blocks):
+            rows = slice(b * P, (b + 1) * P)
             mean_term = blocks.tile([P, N], F32, name="mean_term")
-            nc.vector.tensor_tensor(pair_sum[:], first[:], second[:], ADD)
-            nc.scalar.mul(mean_term[:], pair_sum[:], (1.0 - EMA) / K)
-
-            old_term = blocks.tile([P, N], F32, name="old_term")
-            nc.scalar.mul(old_term[:], stale[:], EMA)
-
-            nc.vector.tensor_tensor(window[:].indirect(offsets[:]), old_term[:], mean_term[:], ADD)
-            nc.sync.dma_start(out[rows, :], window[:])
+            nc.vector.scalar_tensor_tensor(mean_term[:], second[b][:], share, first_share[b][:], MULT, ADD)
+            nc.vector.tensor_tensor(window[b][:].indirect(offsets[:]), old_term[b][:], mean_term[:], ADD)
+            nc.sync.dma_start(out[rows, :], window[b][:])

@@ -1,13 +1,14 @@
 import concourse.mybir as mybir
+from concourse.masks import make_identity
 
 F32 = mybir.dt.float32
 U16 = mybir.dt.uint16
 ADD = mybir.AluOpType.add
-MULT = mybir.AluOpType.mult
 
 P = 128
 D, S, N, K = 256, 4096, 2048, 2
 EMA = 0.99
+BANK = 512
 
 BYTES = 4 * D * (S - N) + 3 * 4 * D * N + 2 * P * (N // 16) + 4 * D * S
 
@@ -15,13 +16,17 @@ BYTES = 4 * D * (S - N) + 3 * 4 * D * N + 2 * P * (N // 16) + 4 * D * S
 def tile_httnbasehead_kernel(tc, base, old, za, zb, offs, out):
     nc = tc.nc
     n_blocks = D // P
+    n_banks = N // BANK
     share = (1.0 - EMA) / K
     with (
         tc.tile_pool(name="held", bufs=1) as held,
         tc.tile_pool(name="blocks", bufs=n_blocks) as blocks,
+        tc.psum_pool(name="banks", bufs=n_banks) as banks,
     ):
         offsets = held.tile([P, N // 16], U16, name="offsets")
         nc.sync.dma_start(offsets[:], offs)
+        identity = held.tile([P, P], F32, name="identity")
+        make_identity(nc, identity[:])
 
         first, second, stale, window = [], [], [], []
         for b in range(n_blocks):
@@ -35,16 +40,26 @@ def tile_httnbasehead_kernel(tc, base, old, za, zb, offs, out):
             nc.sync.dma_start(stale[b][:], old[rows, :])
             nc.sync.dma_start(window[b][:], base[rows, :])
 
-        first_share, old_term = [], []
+        old_term, mean_term = [], []
         for b in range(n_blocks):
-            first_share.append(blocks.tile([P, N], F32, name="first_share"))
             old_term.append(blocks.tile([P, N], F32, name="old_term"))
-            nc.scalar.mul(first_share[b][:], first[b][:], share)
+            mean_term.append(blocks.tile([P, N], F32, name="mean_term"))
             nc.scalar.mul(old_term[b][:], stale[b][:], EMA)
+            if b == 0:
+                pair_sum = held.tile([P, N], F32, name="pair_sum")
+                nc.vector.tensor_tensor(pair_sum[:], first[b][:], second[b][:], ADD)
+                nc.vector.tensor_scalar_mul(mean_term[b][:], pair_sum[:], share)
+            else:
+                bank = [banks.tile([P, BANK], F32, name="bank") for c in range(n_banks)]
+                for c in range(n_banks):
+                    cols = slice(c * BANK, (c + 1) * BANK)
+                    nc.tensor.matmul(bank[c][:], identity[:], first[b][:, cols], start=True, stop=False)
+                for c in range(n_banks):
+                    cols = slice(c * BANK, (c + 1) * BANK)
+                    nc.tensor.matmul(bank[c][:], identity[:], second[b][:, cols], start=False, stop=True)
+                    nc.scalar.mul(mean_term[b][:, cols], bank[c][:], share)
 
         for b in range(n_blocks):
             rows = slice(b * P, (b + 1) * P)
-            mean_term = blocks.tile([P, N], F32, name="mean_term")
-            nc.vector.scalar_tensor_tensor(mean_term[:], second[b][:], share, first_share[b][:], MULT, ADD)
-            nc.vector.tensor_tensor(window[b][:].indirect(offsets[:]), old_term[b][:], mean_term[:], ADD)
+            nc.vector.tensor_tensor(window[b][:].indirect(offsets[:]), old_term[b][:], mean_term[b][:], ADD)
             nc.sync.dma_start(out[rows, :], window[b][:])

@@ -15,12 +15,12 @@ BYTES = 4 * D * (S - N) + 3 * 4 * D * N + 2 * P * (N // 16) + 4 * D * S
 
 def tile_httnbasehead_kernel(tc, base, old, za, zb, offs, out):
     nc = tc.nc
-    n_blocks = D // P
     n_banks = N // BANK
     share = (1.0 - EMA) / K
+    head_rows = slice(0, P)
+    tail_rows = slice(P, 2 * P)
     with (
         tc.tile_pool(name="held", bufs=1) as held,
-        tc.tile_pool(name="blocks", bufs=n_blocks) as blocks,
         tc.psum_pool(name="banks", bufs=n_banks) as banks,
     ):
         offsets = held.tile([P, N // 16], U16, name="offsets")
@@ -28,38 +28,43 @@ def tile_httnbasehead_kernel(tc, base, old, za, zb, offs, out):
         identity = held.tile([P, P], F32, name="identity")
         make_identity(nc, identity[:])
 
-        first, second, stale, window = [], [], [], []
-        for b in range(n_blocks):
-            rows = slice(b * P, (b + 1) * P)
-            first.append(blocks.tile([P, N], F32, name="first"))
-            second.append(blocks.tile([P, N], F32, name="second"))
-            stale.append(blocks.tile([P, N], F32, name="stale"))
-            window.append(blocks.tile([P, S], F32, name="window"))
-            nc.sync.dma_start(first[b][:], za[rows, :])
-            nc.sync.dma_start(second[b][:], zb[rows, :])
-            nc.sync.dma_start(stale[b][:], old[rows, :])
-            nc.sync.dma_start(window[b][:], base[rows, :])
+        head_first = held.tile([P, N], F32, name="head_first")
+        head_second = held.tile([P, N], F32, name="head_second")
+        head_stale = held.tile([P, N], F32, name="head_stale")
+        head_window = held.tile([P, S], F32, name="head_window")
+        nc.sync.dma_start(head_first[:], za[head_rows, :])
+        nc.sync.dma_start(head_second[:], zb[head_rows, :])
+        nc.sync.dma_start(head_stale[:], old[head_rows, :])
+        nc.sync.dma_start(head_window[:], base[head_rows, :])
+        tail_first = held.tile([P, N], F32, name="tail_first")
+        tail_second = held.tile([P, N], F32, name="tail_second")
+        tail_stale = held.tile([P, N], F32, name="tail_stale")
+        tail_window = held.tile([P, S], F32, name="tail_window")
+        for c in range(n_banks):
+            cols = slice(c * BANK, (c + 1) * BANK)
+            nc.sync.dma_start(tail_first[:, cols], za[tail_rows, cols])
+            nc.sync.dma_start(tail_second[:, cols], zb[tail_rows, cols])
+            nc.sync.dma_start(tail_stale[:, cols], old[tail_rows, cols])
+        nc.sync.dma_start(tail_window[:], base[tail_rows, :])
 
-        old_term, mean_term = [], []
-        for b in range(n_blocks):
-            old_term.append(blocks.tile([P, N], F32, name="old_term"))
-            mean_term.append(blocks.tile([P, N], F32, name="mean_term"))
-            nc.scalar.mul(old_term[b][:], stale[b][:], EMA)
-            if b == 0:
-                pair_sum = held.tile([P, N], F32, name="pair_sum")
-                nc.vector.tensor_tensor(pair_sum[:], first[b][:], second[b][:], ADD)
-                nc.vector.tensor_scalar_mul(mean_term[b][:], pair_sum[:], share)
-            else:
-                bank = [banks.tile([P, BANK], F32, name="bank") for c in range(n_banks)]
-                for c in range(n_banks):
-                    cols = slice(c * BANK, (c + 1) * BANK)
-                    nc.tensor.matmul(bank[c][:], identity[:], first[b][:, cols], start=True, stop=False)
-                for c in range(n_banks):
-                    cols = slice(c * BANK, (c + 1) * BANK)
-                    nc.tensor.matmul(bank[c][:], identity[:], second[b][:, cols], start=False, stop=True)
-                    nc.scalar.mul(mean_term[b][:, cols], bank[c][:], share)
+        head_old_term = held.tile([P, N], F32, name="head_old_term")
+        head_pair_sum = held.tile([P, N], F32, name="head_pair_sum")
+        head_mean_term = held.tile([P, N], F32, name="head_mean_term")
+        nc.scalar.mul(head_old_term[:], head_stale[:], EMA)
+        nc.vector.tensor_tensor(head_pair_sum[:], head_first[:], head_second[:], ADD)
+        nc.vector.tensor_scalar_mul(head_mean_term[:], head_pair_sum[:], share)
 
-        for b in range(n_blocks):
-            rows = slice(b * P, (b + 1) * P)
-            nc.vector.tensor_tensor(window[b][:].indirect(offsets[:]), old_term[b][:], mean_term[b][:], ADD)
-            nc.sync.dma_start(out[rows, :], window[b][:])
+        tail_old_term = held.tile([P, N], F32, name="tail_old_term")
+        tail_mean_term = held.tile([P, N], F32, name="tail_mean_term")
+        for c in range(n_banks):
+            cols = slice(c * BANK, (c + 1) * BANK)
+            bank = banks.tile([P, BANK], F32, name="bank")
+            nc.tensor.matmul(bank[:], identity[:], tail_first[:, cols], start=True, stop=False)
+            nc.tensor.matmul(bank[:], identity[:], tail_second[:, cols], start=False, stop=True)
+            nc.scalar.mul(tail_old_term[:, cols], tail_stale[:, cols], EMA)
+            nc.scalar.mul(tail_mean_term[:, cols], bank[:], share)
+
+        nc.vector.tensor_tensor(head_window[:].indirect(offsets[:]), head_old_term[:], head_mean_term[:], ADD)
+        nc.sync.dma_start(out[head_rows, :], head_window[:])
+        nc.vector.tensor_tensor(tail_window[:].indirect(offsets[:]), tail_old_term[:], tail_mean_term[:], ADD)
+        nc.sync.dma_start(out[tail_rows, :], tail_window[:])

@@ -4,6 +4,7 @@ from concourse.masks import make_identity
 F32 = mybir.dt.float32
 U16 = mybir.dt.uint16
 ADD = mybir.AluOpType.add
+MULT = mybir.AluOpType.mult
 
 P = 128
 D, S, N, K = 256, 4096, 2048, 2
@@ -27,6 +28,8 @@ def tile_httnbasehead_kernel(tc, base, old, za, zb, offs, out):
         nc.sync.dma_start(offsets[:], offs)
         identity = held.tile([P, P], F32, name="identity")
         make_identity(nc, identity[:])
+        halving = held.tile([P, P], F32, name="halving")
+        nc.scalar.mul(halving[:], identity[:], 1.0 / K)
 
         head_first = held.tile([P, N], F32, name="head_first")
         head_second = held.tile([P, N], F32, name="head_second")
@@ -40,29 +43,29 @@ def tile_httnbasehead_kernel(tc, base, old, za, zb, offs, out):
         tail_second = held.tile([P, N], F32, name="tail_second")
         tail_stale = held.tile([P, N], F32, name="tail_stale")
         tail_window = held.tile([P, S], F32, name="tail_window")
-        for c in range(n_banks):
-            cols = slice(c * BANK, (c + 1) * BANK)
+        for h in range(2):
+            cols = slice(h * (N // 2), (h + 1) * (N // 2))
             nc.sync.dma_start(tail_first[:, cols], za[tail_rows, cols])
             nc.sync.dma_start(tail_second[:, cols], zb[tail_rows, cols])
             nc.sync.dma_start(tail_stale[:, cols], old[tail_rows, cols])
         nc.sync.dma_start(tail_window[:], base[tail_rows, :])
 
         head_old_term = held.tile([P, N], F32, name="head_old_term")
-        head_pair_sum = held.tile([P, N], F32, name="head_pair_sum")
+        head_first_term = held.tile([P, N], F32, name="head_first_term")
         head_mean_term = held.tile([P, N], F32, name="head_mean_term")
         nc.scalar.mul(head_old_term[:], head_stale[:], EMA)
-        nc.vector.tensor_tensor(head_pair_sum[:], head_first[:], head_second[:], ADD)
-        nc.vector.tensor_scalar_mul(head_mean_term[:], head_pair_sum[:], share)
+        nc.vector.tensor_scalar_mul(head_first_term[:], head_first[:], share)
+        nc.vector.scalar_tensor_tensor(head_mean_term[:], head_second[:], share, head_first_term[:], MULT, ADD)
 
         tail_old_term = held.tile([P, N], F32, name="tail_old_term")
         tail_mean_term = held.tile([P, N], F32, name="tail_mean_term")
         for c in range(n_banks):
             cols = slice(c * BANK, (c + 1) * BANK)
             bank = banks.tile([P, BANK], F32, name="bank")
-            nc.tensor.matmul(bank[:], identity[:], tail_first[:, cols], start=True, stop=False)
-            nc.tensor.matmul(bank[:], identity[:], tail_second[:, cols], start=False, stop=True)
+            nc.tensor.matmul(bank[:], halving[:], tail_first[:, cols], start=True, stop=False)
+            nc.tensor.matmul(bank[:], halving[:], tail_second[:, cols], start=False, stop=True)
             nc.scalar.mul(tail_old_term[:, cols], tail_stale[:, cols], EMA)
-            nc.scalar.mul(tail_mean_term[:, cols], bank[:], share)
+            nc.scalar.mul(tail_mean_term[:, cols], bank[:], 1.0 - EMA)
 
         nc.vector.tensor_tensor(head_window[:].indirect(offsets[:]), head_old_term[:], head_mean_term[:], ADD)
         nc.sync.dma_start(out[head_rows, :], head_window[:])

@@ -67,7 +67,7 @@ def tile_httnbasehead_kernel(tc, base, old, za, zb, offs, out):
             nc.scalar.mul(tail_old_term[:, cols], tail_stale[:, cols], EMA)
             nc.scalar.mul(tail_mean_term[:, cols], bank[:], 1.0 - EMA)
 
-        nc.vector.tensor_tensor(head_window[:].indirect(offsets[:]), head_old_term[:], head_mean_term[:], ADD)
+        nc.vector.tensor_tensor(head_window[:].indirect(offsets[:]), head_mean_term[:], head_old_term[:], ADD)
         nc.sync.dma_start(out[head_rows, :], head_window[:])
-        nc.vector.tensor_tensor(tail_window[:].indirect(offsets[:]), tail_old_term[:], tail_mean_term[:], ADD)
+        nc.vector.tensor_tensor(tail_window[:].indirect(offsets[:]), tail_mean_term[:], tail_old_term[:], ADD)
         nc.sync.dma_start(out[tail_rows, :], tail_window[:])

@@ -10,6 +10,7 @@ P = 128
 D, S, N, K = 256, 4096, 2048, 2
 EMA = 0.99
 BANK = 512
+AXI = 256
 
 BYTES = 4 * D * (S - N) + 3 * 4 * D * N + 2 * P * (N // 16) + 4 * D * S
 
@@ -31,18 +32,18 @@ def tile_httnbasehead_kernel(tc, base, old, za, zb, offs, out):
         halving = held.tile([P, P], F32, name="halving")
         nc.scalar.mul(halving[:], identity[:], 1.0 / K)
 
-        head_first = held.tile([P, N], F32, name="head_first")
-        head_second = held.tile([P, N], F32, name="head_second")
-        head_stale = held.tile([P, N], F32, name="head_stale")
-        head_window = held.tile([P, S], F32, name="head_window")
+        head_first = held.tile([P, N], F32, name="head_first", align_bytes=AXI)
+        head_second = held.tile([P, N], F32, name="head_second", align_bytes=AXI)
+        head_stale = held.tile([P, N], F32, name="head_stale", align_bytes=AXI)
+        head_window = held.tile([P, S], F32, name="head_window", align_bytes=AXI)
         nc.sync.dma_start(head_first[:], za[head_rows, :])
         nc.sync.dma_start(head_second[:], zb[head_rows, :])
         nc.sync.dma_start(head_stale[:], old[head_rows, :])
         nc.sync.dma_start(head_window[:], base[head_rows, :])
-        tail_first = held.tile([P, N], F32, name="tail_first")
-        tail_second = held.tile([P, N], F32, name="tail_second")
-        tail_stale = held.tile([P, N], F32, name="tail_stale")
-        tail_window = held.tile([P, S], F32, name="tail_window")
+        tail_first = held.tile([P, N], F32, name="tail_first", align_bytes=AXI)
+        tail_second = held.tile([P, N], F32, name="tail_second", align_bytes=AXI)
+        tail_stale = held.tile([P, N], F32, name="tail_stale", align_bytes=AXI)
+        tail_window = held.tile([P, S], F32, name="tail_window", align_bytes=AXI)
         for h in range(2):
             cols = slice(h * (N // 2), (h + 1) * (N // 2))
             nc.sync.dma_start(tail_first[:, cols], za[tail_rows, cols])

import concourse.mybir as mybir
from concourse.masks import make_identity

F32 = mybir.dt.float32
U16 = mybir.dt.uint16
ADD = mybir.AluOpType.add
MULT = mybir.AluOpType.mult

P = 128
D, S, N, K = 256, 4096, 2048, 2
EMA = 0.99
BANK = 512
AXI = 256

BYTES = 4 * D * (S - N) + 3 * 4 * D * N + 2 * P * (N // 16) + 4 * D * S


def tile_httnbasehead_kernel(tc, base, old, za, zb, offs, out):
    nc = tc.nc
    n_banks = N // BANK
    share = (1.0 - EMA) / K
    head_rows = slice(0, P)
    tail_rows = slice(P, 2 * P)
    with (
        tc.tile_pool(name="held", bufs=1) as held,
        tc.psum_pool(name="banks", bufs=n_banks) as banks,
    ):
        offsets = held.tile([P, N // 16], U16, name="offsets")
        nc.sync.dma_start(offsets[:], offs)
        identity = held.tile([P, P], F32, name="identity")
        make_identity(nc, identity[:])
        halving = held.tile([P, P], F32, name="halving")
        nc.scalar.mul(halving[:], identity[:], 1.0 / K)

        head_first = held.tile([P, N], F32, name="head_first", align_bytes=AXI)
        head_second = held.tile([P, N], F32, name="head_second", align_bytes=AXI)
        head_stale = held.tile([P, N], F32, name="head_stale", align_bytes=AXI)
        head_window = held.tile([P, S], F32, name="head_window", align_bytes=AXI)
        nc.sync.dma_start(head_first[:], za[head_rows, :])
        nc.sync.dma_start(head_second[:], zb[head_rows, :])
        nc.sync.dma_start(head_stale[:], old[head_rows, :])
        nc.sync.dma_start(head_window[:], base[head_rows, :])
        tail_first = held.tile([P, N], F32, name="tail_first", align_bytes=AXI)
        tail_second = held.tile([P, N], F32, name="tail_second", align_bytes=AXI)
        tail_stale = held.tile([P, N], F32, name="tail_stale", align_bytes=AXI)
        tail_window = held.tile([P, S], F32, name="tail_window", align_bytes=AXI)
        for h in range(2):
            cols = slice(h * (N // 2), (h + 1) * (N // 2))
            nc.sync.dma_start(tail_first[:, cols], za[tail_rows, cols])
            nc.sync.dma_start(tail_second[:, cols], zb[tail_rows, cols])
            nc.sync.dma_start(tail_stale[:, cols], old[tail_rows, cols])
        nc.sync.dma_start(tail_window[:], base[tail_rows, :])

        head_old_term = held.tile([P, N], F32, name="head_old_term")
        head_first_term = held.tile([P, N], F32, name="head_first_term")
        head_mean_term = held.tile([P, N], F32, name="head_mean_term")
        nc.scalar.mul(head_old_term[:], head_stale[:], EMA)
        nc.vector.tensor_scalar_mul(head_first_term[:], head_first[:], share)
        nc.vector.scalar_tensor_tensor(head_mean_term[:], head_second[:], share, head_first_term[:], MULT, ADD)

        tail_old_term = held.tile([P, N], F32, name="tail_old_term")
        tail_mean_term = held.tile([P, N], F32, name="tail_mean_term")
        for c in range(n_banks):
            cols = slice(c * BANK, (c + 1) * BANK)
            bank = banks.tile([P, BANK], F32, name="bank")
            nc.tensor.matmul(bank[:], halving[:], tail_first[:, cols], start=True, stop=False)
            nc.tensor.matmul(bank[:], halving[:], tail_second[:, cols], start=False, stop=True)
            nc.scalar.mul(tail_old_term[:, cols], tail_stale[:, cols], EMA)
            nc.scalar.mul(tail_mean_term[:, cols], bank[:], 1.0 - EMA)

        nc.vector.tensor_tensor(head_window[:].indirect(offsets[:]), head_mean_term[:], head_old_term[:], ADD)
        nc.sync.dma_start(out[head_rows, :], head_window[:])
        nc.vector.tensor_tensor(tail_window[:].indirect(offsets[:]), tail_mean_term[:], tail_old_term[:], ADD)
        nc.sync.dma_start(out[tail_rows, :], tail_window[:])
